import numpy as np
import ml_dtypes

BF16 = ml_dtypes.bfloat16


def bf(x):
    return np.asarray(x, np.float32).astype(BF16)


def f32(x):
    return np.asarray(x, np.float32)


def f64(x):
    return np.asarray(x).astype(np.float64)


def striped(idx):
    return np.tile(idx.reshape(-1, 16).T, (8, 1))


C, S, F, B, T, N = 1024, 256, 64, 4, 256, 1024
TSTEP = 1.0


def setup_inputs():
    return {"x": f32(np.random.standard_normal((C, S))), "amp": f32(np.sqrt(2.0 / F) * np.random.standard_normal((C, F))), "freq": f32(np.random.uniform(0.05, 0.45, (1, F))), "offs": striped(np.concatenate([np.random.permutation(S) for _ in range(B)]))}


def reference(x, amp, freq, offs):
    idx = offs[:16].T.reshape(-1)
    th = 2.0 * np.pi * f64(freq)[0] * TSTEP
    p = (f64(amp) * np.cos(th)[None, :]).sum(axis=1, keepdims=True)
    q = (f64(amp) * np.sin(th)[None, :]).sum(axis=1, keepdims=True)
    ang = 2.0 * np.pi * (np.arange(N) % T) / T
    coef = p * np.cos(ang)[None, :] + q * np.sin(ang)[None, :]
    return f64(x)[:, idx] * coef

@@ -1,0 +1,120 @@
+import concourse.mybir as mybir
+from concourse.masks import make_identity
+
+F32 = mybir.dt.float32
+I32 = mybir.dt.int32
+U16 = mybir.dt.uint16
+U32 = mybir.dt.uint32
+ALU = mybir.AluOpType
+ACT = mybir.ActivationFunctionType
+
+P = 128
+C, S, F, N = 1024, 256, 64, 1024
+BLOCKS = C // P
+PIECES = N // S
+QUARTER = S // 4
+EARLY = 2
+
+TWO_PI = 6.283185
+TURN = 1 << 22
+
+FLOPS = 2 * C * F * S + C * N
+
+
+def tile_waveencoder_kernel(tc, x, amp, freq, offs, out):
+    nc = tc.nc
+    with (
+        tc.tile_pool(name="held", bufs=1) as held,
+        tc.tile_pool(name="products", bufs=8) as products,
+        tc.psum_pool(name="flipped", bufs=2) as flipped,
+        tc.psum_pool(name="sums", bufs=3) as sums,
+    ):
+        identity = held.tile([P, P], F32, name="identity")
+        nc.vector.memset(identity[:], 0.0)
+        make_identity(nc, identity[:], nomemset=True)
+
+        freq_col = held.tile([F, 1], F32, name="freq_col")
+        with nc.allow_non_contiguous_dma(reason="64 frequencies, one to a partition"):
+            nc.sync.dma_start(freq_col[:], freq.rearrange("o m -> m o"))
+        offsets = held.tile([P, N // 16], U16, name="offsets")
+        nc.sync.dma_start(offsets[:], offs)
+        amp_wide = held.tile([P, BLOCKS, 2 * F], F32, name="amp_wide")
+        amp_blocks = amp.rearrange("(b p) m -> p b m", p=P)
+        nc.vector.memset(amp_wide[:, :, F : 2 * F], 0.0)
+        nc.scalar.dma_start(amp_wide[:, 0:EARLY, 0:F], amp_blocks[:, 0:EARLY, :])
+        nc.sync.dma_start(amp_wide[:, EARLY:BLOCKS, 0:F], amp_blocks[:, EARLY:BLOCKS, :])
+        tables = []
+        for b in range(BLOCKS):
+            table = held.tile([P, S], F32, name=f"table{b}")
+            queue = nc.scalar if b == 0 else nc.sync
+            queue.dma_start(table[:], x[b * P : (b + 1) * P, :])
+            tables.append(table)
+
+        position = held.tile([P, S + QUARTER], F32, name="position")
+        nc.gpsimd.iota(position[:, 0 : S // 2], pattern=[[1, S // 2]], base=0, channel_multiplier=0,
+                       allow_small_or_imprecise_dtypes=True)
+        nc.gpsimd.iota(position[:, S // 2 :], pattern=[[1, S // 2 + QUARTER]], base=-(S // 2), channel_multiplier=0,
+                       allow_small_or_imprecise_dtypes=True)
+        sine = held.tile([P, S + QUARTER], F32, name="sine")
+        nc.scalar.activation(out=sine[:], in_=position[:], func=ACT.Sin, scale=TWO_PI / S)
+        sin_a = sine[:, 0:S]
+        cos_a = sine[:, QUARTER : QUARTER + S]
+        phase = held.tile([F, 2], F32, name="phase")
+        nc.vector.memset(phase[:, 0:1], float(3 * TURN // 4))
+        nc.vector.memset(phase[:, 1:2], float(TURN // 2))
+        minus_half_turn = held.tile([F, 1], F32, name="minus_half_turn")
+        nc.vector.memset(minus_half_turn[:], -TWO_PI / 2)
+        cos_sin_th = held.tile([P, 2], F32, name="cos_sin_th")
+        nc.vector.memset(cos_sin_th[F:P, :], 0.0)
+        wave = held.tile([P, S], F32, name="wave")
+        nc.vector.memset(wave[F:P, :], 0.0)
+
+        turns = held.tile([F, 2], I32, name="turns")
+        nc.vector.scalar_tensor_tensor(out=turns[:], in0=freq_col[:, 0:1].to_broadcast([F, 2]), scalar=float(TURN),
+                                       in1=phase[:], op0=ALU.mult, op1=ALU.add)
+        fraction = held.tile([F, 2], I32, name="fraction")
+        nc.vector.tensor_scalar(out=fraction[:], in0=turns[:], scalar1=TURN - 1, scalar2=None, op0=ALU.bitwise_and)
+        nc.scalar.activation(out=cos_sin_th[0:F, :], in_=fraction[:].bitcast(U32), func=ACT.Sin, scale=TWO_PI / TURN,
+                             bias=minus_half_turn[:])
+
+        def flip_amp(b):
+            amp_t_psum = flipped.tile([P, P], F32, name="amp_t_psum")
+            nc.tensor.transpose(out=amp_t_psum[:], in_=amp_wide[:, b, :], identity=identity[:])
+            amp_t = held.tile([P, P], F32, name=f"amp_t{b}")
+            nc.scalar.copy(out=amp_t[:], in_=amp_t_psum[:])
+            return amp_t
+
+        p_q = flipped.tile([P, 2], F32, name="p_q")
+        nc.tensor.matmul(out=p_q[:], lhsT=flip_amp(0)[:], rhs=cos_sin_th[:], start=True, stop=True)
+
+        cos_part = held.tile([F, S], F32, name="cos_part")
+        nc.vector.tensor_scalar(out=cos_part[:], in0=cos_a[0:F, :], scalar1=cos_sin_th[0:F, 0:1], scalar2=None, op0=ALU.mult)
+        nc.vector.scalar_tensor_tensor(out=wave[0:F, :], in0=sin_a[0:F, :], scalar=cos_sin_th[0:F, 1:2], in1=cos_part[:],
+                                       op0=ALU.mult, op1=ALU.add)
+
+        coefs = []
+        p_cos = held.tile([P, S], F32, name="p_cos")
+        nc.vector.tensor_scalar(out=p_cos[:], in0=cos_a, scalar1=p_q[:, 0:1], scalar2=None, op0=ALU.mult)
+        coef = held.tile([P, S], F32, name="coef0")
+        nc.vector.scalar_tensor_tensor(out=coef[:], in0=sin_a, scalar=p_q[:, 1:2], in1=p_cos[:], op0=ALU.mult, op1=ALU.add)
+        coefs.append(coef)
+
+        for b in range(1, BLOCKS):
+            coef_psum = sums.tile([P, S], F32, name="coef_psum")
+            nc.tensor.matmul(out=coef_psum[:], lhsT=flip_amp(b)[:], rhs=wave[:], start=True, stop=True)
+            coef = held.tile([P, S], F32, name=f"coef{b}")
+            nc.scalar.copy(out=coef[:], in_=coef_psum[:])
+            coefs.append(coef)
+
+        for b in range(BLOCKS):
+            widths = [N] if b < BLOCKS - 1 else [S, S, S, S // 2, S // 2]
+            start = 0
+            for width in widths:
+                product = products.tile([P, width], F32, name="product")
+                for j in range(start, start + width, S):
+                    n = min(S, width)
+                    picked = tables[b][:].indirect(offsets[:, j // 16 : (j + n) // 16])
+                    nc.vector.tensor_tensor(out=product[:, j - start : j - start + n], in0=picked,
+                                            in1=coefs[b][:, j % S : j % S + n], op=ALU.mult)
+                nc.sync.dma_start(out[b * P : (b + 1) * P, start : start + width], product[:])
+                start += width

@@ -2,21 +2,19 @@ import concourse.mybir as mybir
 from concourse.masks import make_identity
 
 F32 = mybir.dt.float32
-I32 = mybir.dt.int32
 U16 = mybir.dt.uint16
-U32 = mybir.dt.uint32
 ALU = mybir.AluOpType
 ACT = mybir.ActivationFunctionType
 
 P = 128
 C, S, F, N = 1024, 256, 64, 1024
+HALF, QUARTER = S // 2, S // 4
 BLOCKS = C // P
-PIECES = N // S
-QUARTER = S // 4
+SQUARE = 32
+HALVES_F = F // SQUARE
 EARLY = 2
 
 TWO_PI = 6.283185
-TURN = 1 << 22
 
 FLOPS = 2 * C * F * S + C * N
 
@@ -29,92 +27,95 @@ def tile_waveencoder_kernel(tc, x, amp, freq, offs, out):
         tc.psum_pool(name="flipped", bufs=2) as flipped,
         tc.psum_pool(name="sums", bufs=3) as sums,
     ):
-        identity = held.tile([P, P], F32, name="identity")
-        nc.vector.memset(identity[:], 0.0)
-        make_identity(nc, identity[:], nomemset=True)
-
-        freq_col = held.tile([F, 1], F32, name="freq_col")
-        with nc.allow_non_contiguous_dma(reason="64 frequencies, one to a partition"):
-            nc.sync.dma_start(freq_col[:], freq.rearrange("o m -> m o"))
-        offsets = held.tile([P, N // 16], U16, name="offsets")
-        nc.sync.dma_start(offsets[:], offs)
+        freq_rows = held.tile([P, F], F32, name="freq_rows", align_bytes=64)
+        nc.gpsimd.memset(freq_rows[:], 0.0)
+        nc.sync.dma_start(freq_rows[0:P:SQUARE, :], freq.to_broadcast([P // SQUARE, F]))
         amp_wide = held.tile([P, BLOCKS, 2 * F], F32, name="amp_wide")
         amp_blocks = amp.rearrange("(b p) m -> p b m", p=P)
-        nc.vector.memset(amp_wide[:, :, F : 2 * F], 0.0)
-        nc.scalar.dma_start(amp_wide[:, 0:EARLY, 0:F], amp_blocks[:, 0:EARLY, :])
-        nc.sync.dma_start(amp_wide[:, EARLY:BLOCKS, 0:F], amp_blocks[:, EARLY:BLOCKS, :])
+        nc.sync.dma_start(amp_wide[:, 0:EARLY, 0:F], amp_blocks[:, 0:EARLY, :])
+        offsets = held.tile([P, N // 16], U16, name="offsets")
+        nc.sync.dma_start(offsets[:], offs)
         tables = []
         for b in range(BLOCKS):
             table = held.tile([P, S], F32, name=f"table{b}")
-            queue = nc.scalar if b == 0 else nc.sync
-            queue.dma_start(table[:], x[b * P : (b + 1) * P, :])
+            nc.sync.dma_start(table[:], x[b * P : (b + 1) * P, :])
             tables.append(table)
+            if b == 0:
+                nc.sync.dma_start(amp_wide[:, EARLY:BLOCKS, 0:F], amp_blocks[:, EARLY:BLOCKS, :])
 
-        position = held.tile([P, S + QUARTER], F32, name="position")
-        nc.gpsimd.iota(position[:, 0 : S // 2], pattern=[[1, S // 2]], base=0, channel_multiplier=0,
+        position = held.tile([P, HALF + QUARTER], F32, name="position")
+        nc.gpsimd.iota(position[:], pattern=[[1, HALF + QUARTER]], base=-QUARTER, channel_multiplier=0,
                        allow_small_or_imprecise_dtypes=True)
-        nc.gpsimd.iota(position[:, S // 2 :], pattern=[[1, S // 2 + QUARTER]], base=-(S // 2), channel_multiplier=0,
-                       allow_small_or_imprecise_dtypes=True)
-        sine = held.tile([P, S + QUARTER], F32, name="sine")
+        sine = held.tile([P, HALF + QUARTER], F32, name="sine")
         nc.scalar.activation(out=sine[:], in_=position[:], func=ACT.Sin, scale=TWO_PI / S)
-        sin_a = sine[:, 0:S]
-        cos_a = sine[:, QUARTER : QUARTER + S]
-        phase = held.tile([F, 2], F32, name="phase")
-        nc.vector.memset(phase[:, 0:1], float(3 * TURN // 4))
-        nc.vector.memset(phase[:, 1:2], float(TURN // 2))
-        minus_half_turn = held.tile([F, 1], F32, name="minus_half_turn")
-        nc.vector.memset(minus_half_turn[:], -TWO_PI / 2)
-        cos_sin_th = held.tile([P, 2], F32, name="cos_sin_th")
-        nc.vector.memset(cos_sin_th[F:P, :], 0.0)
+        minus_cos_a = sine[:, 0:HALF]
+        sin_a = sine[:, QUARTER : QUARTER + HALF]
+        minus_quarter_turn = held.tile([P, 1], F32, name="minus_quarter_turn")
+        nc.vector.memset(minus_quarter_turn[:], -TWO_PI / 4)
+        identity = held.tile([P, P], F32, name="identity")
+        nc.vector.memset(identity[:], 0.0)
+        make_identity(nc, identity[:], nomemset=True)
+        nc.vector.memset(amp_wide[:, :, F : 2 * F], 0.0)
         wave = held.tile([P, S], F32, name="wave")
         nc.vector.memset(wave[F:P, :], 0.0)
 
-        turns = held.tile([F, 2], I32, name="turns")
-        nc.vector.scalar_tensor_tensor(out=turns[:], in0=freq_col[:, 0:1].to_broadcast([F, 2]), scalar=float(TURN),
-                                       in1=phase[:], op0=ALU.mult, op1=ALU.add)
-        fraction = held.tile([F, 2], I32, name="fraction")
-        nc.vector.tensor_scalar(out=fraction[:], in0=turns[:], scalar1=TURN - 1, scalar2=None, op0=ALU.bitwise_and)
-        nc.scalar.activation(out=cos_sin_th[0:F, :], in_=fraction[:].bitcast(U32), func=ACT.Sin, scale=TWO_PI / TURN,
-                             bias=minus_half_turn[:])
+        freq_cols = held.tile([P, HALVES_F, SQUARE], F32, name="freq_cols", align_bytes=64)
+        for h in range(HALVES_F):
+            nc.vector.transpose(freq_cols[:, h, :], freq_rows[:, h * SQUARE : (h + 1) * SQUARE])
+        trig_cols = held.tile([P, 2, HALVES_F, SQUARE], F32, name="trig_cols", align_bytes=64)
+        spread = freq_cols[:, :, 0:1].to_broadcast([P, HALVES_F, SQUARE])
+        nc.scalar.activation(out=trig_cols[:, 0], in_=spread, func=ACT.Sin, scale=TWO_PI, bias=minus_quarter_turn[:])
+        nc.scalar.activation(out=trig_cols[:, 1], in_=spread, func=ACT.Sin, scale=TWO_PI)
+        trig = held.tile([P, 2 * F], F32, name="trig", align_bytes=64)
+        nc.vector.transpose(trig[:], trig_cols[:].rearrange("p k h i -> p (k h i)"))
+        minus_p_q = held.tile([P, 2], F32, name="minus_p_q")
+        terms = held.tile([P, 2, F], F32, name="terms")
+        for k in range(2):
+            nc.vector.scalar_tensor_tensor(out=terms[:, k, :], in0=amp_wide[:, 0, 0:F], scalar=1.0, in1=trig[:, k * F : (k + 1) * F],
+                                           op0=ALU.mult, op1=ALU.mult, accum_out=minus_p_q[:, k : k + 1])
+        p_cos = held.tile([P, HALF], F32, name="p_cos")
+        nc.vector.tensor_scalar(out=p_cos[:], in0=minus_cos_a, scalar1=minus_p_q[:, 0:1], scalar2=None, op0=ALU.mult)
+        coefs = [held.tile([P, S], F32, name="coef0")]
+        nc.vector.scalar_tensor_tensor(out=coefs[0][:, 0:HALF], in0=sin_a, scalar=minus_p_q[:, 1:2], in1=p_cos[:],
+                                       op0=ALU.mult, op1=ALU.add)
+        nc.scalar.mul(coefs[0][:, HALF:S], coefs[0][:, 0:HALF], -1.0)
 
-        def flip_amp(b):
+        th_col = held.tile([F, 2], F32, name="th_col")
+        for h in range(HALVES_F):
+            rows = slice(h * SQUARE, (h + 1) * SQUARE)
+            for k, factor in enumerate((-TWO_PI, TWO_PI)):
+                nc.vector.tensor_scalar(out=th_col[rows, k : k + 1], in0=freq_cols[rows, h, 0:1], scalar1=factor, scalar2=None,
+                                        op0=ALU.mult)
+        t = position[0:F, QUARTER:]
+        for s, width, start, sign in ((0, QUARTER, QUARTER, 1), (QUARTER, HALF, 0, -1), (QUARTER + HALF, QUARTER, 0, 1)):
+            nc.scalar.activation(out=wave[0:F, s : s + width], in_=t[:, start : start + width], func=ACT.Sin,
+                                 scale=sign * TWO_PI / S, bias=th_col[:, 0:1] if sign > 0 else th_col[:, 1:2])
+
+        for b in range(1, BLOCKS):
             amp_t_psum = flipped.tile([P, P], F32, name="amp_t_psum")
             nc.tensor.transpose(out=amp_t_psum[:], in_=amp_wide[:, b, :], identity=identity[:])
             amp_t = held.tile([P, P], F32, name=f"amp_t{b}")
             nc.scalar.copy(out=amp_t[:], in_=amp_t_psum[:])
-            return amp_t
-
-        p_q = flipped.tile([P, 2], F32, name="p_q")
-        nc.tensor.matmul(out=p_q[:], lhsT=flip_amp(0)[:], rhs=cos_sin_th[:], start=True, stop=True)
-
-        cos_part = held.tile([F, S], F32, name="cos_part")
-        nc.vector.tensor_scalar(out=cos_part[:], in0=cos_a[0:F, :], scalar1=cos_sin_th[0:F, 0:1], scalar2=None, op0=ALU.mult)
-        nc.vector.scalar_tensor_tensor(out=wave[0:F, :], in0=sin_a[0:F, :], scalar=cos_sin_th[0:F, 1:2], in1=cos_part[:],
-                                       op0=ALU.mult, op1=ALU.add)
-
-        coefs = []
-        p_cos = held.tile([P, S], F32, name="p_cos")
-        nc.vector.tensor_scalar(out=p_cos[:], in0=cos_a, scalar1=p_q[:, 0:1], scalar2=None, op0=ALU.mult)
-        coef = held.tile([P, S], F32, name="coef0")
-        nc.vector.scalar_tensor_tensor(out=coef[:], in0=sin_a, scalar=p_q[:, 1:2], in1=p_cos[:], op0=ALU.mult, op1=ALU.add)
-        coefs.append(coef)
-
-        for b in range(1, BLOCKS):
             coef_psum = sums.tile([P, S], F32, name="coef_psum")
-            nc.tensor.matmul(out=coef_psum[:], lhsT=flip_amp(b)[:], rhs=wave[:], start=True, stop=True)
+            nc.tensor.matmul(out=coef_psum[:], lhsT=amp_t[:], rhs=wave[:], start=True, stop=True)
             coef = held.tile([P, S], F32, name=f"coef{b}")
             nc.scalar.copy(out=coef[:], in_=coef_psum[:])
             coefs.append(coef)
 
+        def look_up(b, product, start, j, n):
+            nc.vector.tensor_tensor(out=product[:, j - start : j - start + n],
+                                    in0=tables[b][:].indirect(offsets[:, j // 16 : (j + n) // 16]),
+                                    in1=coefs[b][:, j % S : j % S + n], op=ALU.mult)
+
         for b in range(BLOCKS):
-            widths = [N] if b < BLOCKS - 1 else [S, S, S, S // 2, S // 2]
+            widths = [N] if b < BLOCKS - 1 else [S, S, S, HALF, HALF]
             start = 0
             for width in widths:
                 product = products.tile([P, width], F32, name="product")
-                for j in range(start, start + width, S):
-                    n = min(S, width)
-                    picked = tables[b][:].indirect(offsets[:, j // 16 : (j + n) // 16])
-                    nc.vector.tensor_tensor(out=product[:, j - start : j - start + n], in0=picked,
-                                            in1=coefs[b][:, j % S : j % S + n], op=ALU.mult)
+                pieces = [(j, min(S, width)) for j in range(start, start + width, S)]
+                if b == 0:
+                    pieces = [(0, HALF), (S, HALF), (HALF, HALF), (S + HALF, HALF), *pieces[2:]]
+                for j, n in pieces:
+                    look_up(b, product, start, j, n)
                 nc.sync.dma_start(out[b * P : (b + 1) * P, start : start + width], product[:])
                 start += width

@@ -10,8 +10,6 @@ P = 128
 C, S, F, N = 1024, 256, 64, 1024
 HALF, QUARTER = S // 2, S // 4
 BLOCKS = C // P
-SQUARE = 32
-HALVES_F = F // SQUARE
 EARLY = 2
 
 TWO_PI = 6.283185
@@ -27,9 +25,9 @@ def tile_waveencoder_kernel(tc, x, amp, freq, offs, out):
         tc.psum_pool(name="flipped", bufs=2) as flipped,
         tc.psum_pool(name="sums", bufs=3) as sums,
     ):
-        freq_rows = held.tile([P, F], F32, name="freq_rows", align_bytes=64)
-        nc.gpsimd.memset(freq_rows[:], 0.0)
-        nc.sync.dma_start(freq_rows[0:P:SQUARE, :], freq.to_broadcast([P // SQUARE, F]))
+        freq_col = held.tile([F, 1], F32, name="freq_col")
+        with nc.allow_non_contiguous_dma(reason="64 frequencies, one to a partition"):
+            nc.sync.dma_start(freq_col[:], freq.rearrange("o m -> m o"))
         amp_wide = held.tile([P, BLOCKS, 2 * F], F32, name="amp_wide")
         amp_blocks = amp.rearrange("(b p) m -> p b m", p=P)
         nc.sync.dma_start(amp_wide[:, 0:EARLY, 0:F], amp_blocks[:, 0:EARLY, :])
@@ -43,63 +41,55 @@ def tile_waveencoder_kernel(tc, x, amp, freq, offs, out):
             if b == 0:
                 nc.sync.dma_start(amp_wide[:, EARLY:BLOCKS, 0:F], amp_blocks[:, EARLY:BLOCKS, :])
 
-        position = held.tile([P, HALF + QUARTER], F32, name="position")
-        nc.gpsimd.iota(position[:], pattern=[[1, HALF + QUARTER]], base=-QUARTER, channel_multiplier=0,
+        position = held.tile([P, S + QUARTER], F32, name="position")
+        nc.gpsimd.iota(position[:, 0 : QUARTER + HALF], pattern=[[1, QUARTER + HALF]], base=-QUARTER, channel_multiplier=0,
                        allow_small_or_imprecise_dtypes=True)
-        sine = held.tile([P, HALF + QUARTER], F32, name="sine")
+        nc.gpsimd.iota(position[:, QUARTER + HALF :], pattern=[[1, HALF]], base=-HALF, channel_multiplier=0,
+                       allow_small_or_imprecise_dtypes=True)
+        sine = held.tile([P, S + QUARTER], F32, name="sine")
         nc.scalar.activation(out=sine[:], in_=position[:], func=ACT.Sin, scale=TWO_PI / S)
-        minus_cos_a = sine[:, 0:HALF]
-        sin_a = sine[:, QUARTER : QUARTER + HALF]
+        minus_cos_a = sine[:, 0:S]
+        sin_a = sine[:, QUARTER : QUARTER + S]
         minus_quarter_turn = held.tile([P, 1], F32, name="minus_quarter_turn")
         nc.vector.memset(minus_quarter_turn[:], -TWO_PI / 4)
         identity = held.tile([P, P], F32, name="identity")
         nc.vector.memset(identity[:], 0.0)
         make_identity(nc, identity[:], nomemset=True)
         nc.vector.memset(amp_wide[:, :, F : 2 * F], 0.0)
-        wave = held.tile([P, S], F32, name="wave")
+        wave = held.tile([P, HALF], F32, name="wave")
         nc.vector.memset(wave[F:P, :], 0.0)
 
-        freq_cols = held.tile([P, HALVES_F, SQUARE], F32, name="freq_cols", align_bytes=64)
-        for h in range(HALVES_F):
-            nc.vector.transpose(freq_cols[:, h, :], freq_rows[:, h * SQUARE : (h + 1) * SQUARE])
-        trig_cols = held.tile([P, 2, HALVES_F, SQUARE], F32, name="trig_cols", align_bytes=64)
-        spread = freq_cols[:, :, 0:1].to_broadcast([P, HALVES_F, SQUARE])
-        nc.scalar.activation(out=trig_cols[:, 0], in_=spread, func=ACT.Sin, scale=TWO_PI, bias=minus_quarter_turn[:])
-        nc.scalar.activation(out=trig_cols[:, 1], in_=spread, func=ACT.Sin, scale=TWO_PI)
-        trig = held.tile([P, 2 * F], F32, name="trig", align_bytes=64)
-        nc.vector.transpose(trig[:], trig_cols[:].rearrange("p k h i -> p (k h i)"))
+        freq_all = flipped.tile([P, F], F32, name="freq_all")
+        nc.tensor.transpose(out=freq_all[:], in_=freq_col[:].to_broadcast([F, P]), identity=identity[0:F, 0:F])
+        trig = held.tile([P, 2, F], F32, name="trig")
+        nc.scalar.activation(out=trig[:, 0, :], in_=freq_all[:], func=ACT.Sin, scale=TWO_PI, bias=minus_quarter_turn[:])
+        nc.scalar.activation(out=trig[:, 1, :], in_=freq_all[:], func=ACT.Sin, scale=TWO_PI)
         minus_p_q = held.tile([P, 2], F32, name="minus_p_q")
         terms = held.tile([P, 2, F], F32, name="terms")
         for k in range(2):
-            nc.vector.scalar_tensor_tensor(out=terms[:, k, :], in0=amp_wide[:, 0, 0:F], scalar=1.0, in1=trig[:, k * F : (k + 1) * F],
+            nc.vector.scalar_tensor_tensor(out=terms[:, k, :], in0=amp_wide[:, 0, 0:F], scalar=1.0, in1=trig[:, k, :],
                                            op0=ALU.mult, op1=ALU.mult, accum_out=minus_p_q[:, k : k + 1])
-        p_cos = held.tile([P, HALF], F32, name="p_cos")
+        p_cos = held.tile([P, S], F32, name="p_cos")
         nc.vector.tensor_scalar(out=p_cos[:], in0=minus_cos_a, scalar1=minus_p_q[:, 0:1], scalar2=None, op0=ALU.mult)
         coefs = [held.tile([P, S], F32, name="coef0")]
-        nc.vector.scalar_tensor_tensor(out=coefs[0][:, 0:HALF], in0=sin_a, scalar=minus_p_q[:, 1:2], in1=p_cos[:],
+        nc.vector.scalar_tensor_tensor(out=coefs[0][:], in0=sin_a, scalar=minus_p_q[:, 1:2], in1=p_cos[:],
                                        op0=ALU.mult, op1=ALU.add)
-        nc.scalar.mul(coefs[0][:, HALF:S], coefs[0][:, 0:HALF], -1.0)
 
-        th_col = held.tile([F, 2], F32, name="th_col")
-        for h in range(HALVES_F):
-            rows = slice(h * SQUARE, (h + 1) * SQUARE)
-            for k, factor in enumerate((-TWO_PI, TWO_PI)):
-                nc.vector.tensor_scalar(out=th_col[rows, k : k + 1], in0=freq_cols[rows, h, 0:1], scalar1=factor, scalar2=None,
-                                        op0=ALU.mult)
-        t = position[0:F, QUARTER:]
-        for s, width, start, sign in ((0, QUARTER, QUARTER, 1), (QUARTER, HALF, 0, -1), (QUARTER + HALF, QUARTER, 0, 1)):
-            nc.scalar.activation(out=wave[0:F, s : s + width], in_=t[:, start : start + width], func=ACT.Sin,
-                                 scale=sign * TWO_PI / S, bias=th_col[:, 0:1] if sign > 0 else th_col[:, 1:2])
+        minus_th = held.tile([F, 1], F32, name="minus_th")
+        nc.gpsimd.tensor_scalar(out=minus_th[:], in0=freq_col[:], scalar1=-TWO_PI, scalar2=None, op0=ALU.mult)
+        nc.scalar.activation(out=wave[0:F, :], in_=position[0:F, QUARTER : QUARTER + HALF], func=ACT.Sin, scale=TWO_PI / S, bias=minus_th[:])
 
         for b in range(1, BLOCKS):
             amp_t_psum = flipped.tile([P, P], F32, name="amp_t_psum")
             nc.tensor.transpose(out=amp_t_psum[:], in_=amp_wide[:, b, :], identity=identity[:])
             amp_t = held.tile([P, P], F32, name=f"amp_t{b}")
             nc.scalar.copy(out=amp_t[:], in_=amp_t_psum[:])
-            coef_psum = sums.tile([P, S], F32, name="coef_psum")
+            coef_psum = sums.tile([P, HALF], F32, name="coef_psum")
             nc.tensor.matmul(out=coef_psum[:], lhsT=amp_t[:], rhs=wave[:], start=True, stop=True)
             coef = held.tile([P, S], F32, name=f"coef{b}")
-            nc.scalar.copy(out=coef[:], in_=coef_psum[:])
+            nc.scalar.copy(out=coef[:, 0:QUARTER], in_=coef_psum[:, QUARTER:HALF])
+            nc.scalar.mul(coef[:, QUARTER : QUARTER + HALF], coef_psum[:], -1.0)
+            nc.scalar.copy(out=coef[:, QUARTER + HALF : S], in_=coef_psum[:, 0:QUARTER])
             coefs.append(coef)
 
         def look_up(b, product, start, j, n):
@@ -112,10 +102,7 @@ def tile_waveencoder_kernel(tc, x, amp, freq, offs, out):
             start = 0
             for width in widths:
                 product = products.tile([P, width], F32, name="product")
-                pieces = [(j, min(S, width)) for j in range(start, start + width, S)]
-                if b == 0:
-                    pieces = [(0, HALF), (S, HALF), (HALF, HALF), (S + HALF, HALF), *pieces[2:]]
-                for j, n in pieces:
-                    look_up(b, product, start, j, n)
+                for j in range(start, start + width, S):
+                    look_up(b, product, start, j, min(S, width))
                 nc.sync.dma_start(out[b * P : (b + 1) * P, start : start + width], product[:])
                 start += width

@@ -41,6 +41,9 @@ def tile_waveencoder_kernel(tc, x, amp, freq, offs, out):
             if b == 0:
                 nc.sync.dma_start(amp_wide[:, EARLY:BLOCKS, 0:F], amp_blocks[:, EARLY:BLOCKS, :])
 
+        identity = held.tile([P, P], F32, name="identity")
+        nc.vector.memset(identity[:], 0.0)
+        make_identity(nc, identity[:], nomemset=True)
         position = held.tile([P, S + QUARTER], F32, name="position")
         nc.gpsimd.iota(position[:, 0 : QUARTER + HALF], pattern=[[1, QUARTER + HALF]], base=-QUARTER, channel_multiplier=0,
                        allow_small_or_imprecise_dtypes=True)
@@ -52,9 +55,6 @@ def tile_waveencoder_kernel(tc, x, amp, freq, offs, out):
         sin_a = sine[:, QUARTER : QUARTER + S]
         minus_quarter_turn = held.tile([P, 1], F32, name="minus_quarter_turn")
         nc.vector.memset(minus_quarter_turn[:], -TWO_PI / 4)
-        identity = held.tile([P, P], F32, name="identity")
-        nc.vector.memset(identity[:], 0.0)
-        make_identity(nc, identity[:], nomemset=True)
         nc.vector.memset(amp_wide[:, :, F : 2 * F], 0.0)
         wave = held.tile([P, HALF], F32, name="wave")
         nc.vector.memset(wave[F:P, :], 0.0)
@@ -70,10 +70,13 @@ def tile_waveencoder_kernel(tc, x, amp, freq, offs, out):
             nc.vector.scalar_tensor_tensor(out=terms[:, k, :], in0=amp_wide[:, 0, 0:F], scalar=1.0, in1=trig[:, k, :],
                                            op0=ALU.mult, op1=ALU.mult, accum_out=minus_p_q[:, k : k + 1])
         p_cos = held.tile([P, S], F32, name="p_cos")
-        nc.vector.tensor_scalar(out=p_cos[:], in0=minus_cos_a, scalar1=minus_p_q[:, 0:1], scalar2=None, op0=ALU.mult)
         coefs = [held.tile([P, S], F32, name="coef0")]
-        nc.vector.scalar_tensor_tensor(out=coefs[0][:], in0=sin_a, scalar=minus_p_q[:, 1:2], in1=p_cos[:],
-                                       op0=ALU.mult, op1=ALU.add)
+        halves = (slice(0, HALF), slice(HALF, S))
+        for half in halves:
+            nc.vector.tensor_scalar(out=p_cos[:, half], in0=minus_cos_a[:, half], scalar1=minus_p_q[:, 0:1], scalar2=None, op0=ALU.mult)
+        for half in halves:
+            nc.vector.scalar_tensor_tensor(out=coefs[0][:, half], in0=sin_a[:, half], scalar=minus_p_q[:, 1:2], in1=p_cos[:, half],
+                                           op0=ALU.mult, op1=ALU.add)
 
         minus_th = held.tile([F, 1], F32, name="minus_th")
         nc.gpsimd.tensor_scalar(out=minus_th[:], in0=freq_col[:], scalar1=-TWO_PI, scalar2=None, op0=ALU.mult)
@@ -102,7 +105,10 @@ def tile_waveencoder_kernel(tc, x, amp, freq, offs, out):
             start = 0
             for width in widths:
                 product = products.tile([P, width], F32, name="product")
-                for j in range(start, start + width, S):
-                    look_up(b, product, start, j, min(S, width))
+                pieces = [(j, min(S, width)) for j in range(start, start + width, S)]
+                if b == 0:
+                    pieces = [(0, HALF), (S, HALF), (HALF, HALF), (S + HALF, HALF), *pieces[2:]]
+                for j, n in pieces:
+                    look_up(b, product, start, j, n)
                 nc.sync.dma_start(out[b * P : (b + 1) * P, start : start + width], product[:])
                 start += width

import concourse.mybir as mybir
from concourse.masks import make_identity

F32 = mybir.dt.float32
U16 = mybir.dt.uint16
ALU = mybir.AluOpType
ACT = mybir.ActivationFunctionType

P = 128
C, S, F, N = 1024, 256, 64, 1024
HALF, QUARTER = S // 2, S // 4
BLOCKS = C // P
EARLY = 2

TWO_PI = 6.283185

FLOPS = 2 * C * F * S + C * N


def tile_waveencoder_kernel(tc, x, amp, freq, offs, out):
    nc = tc.nc
    with (
        tc.tile_pool(name="held", bufs=1) as held,
        tc.tile_pool(name="products", bufs=8) as products,
        tc.psum_pool(name="flipped", bufs=2) as flipped,
        tc.psum_pool(name="sums", bufs=3) as sums,
    ):
        freq_col = held.tile([F, 1], F32, name="freq_col")
        with nc.allow_non_contiguous_dma(reason="64 frequencies, one to a partition"):
            nc.sync.dma_start(freq_col[:], freq.rearrange("o m -> m o"))
        amp_wide = held.tile([P, BLOCKS, 2 * F], F32, name="amp_wide")
        amp_blocks = amp.rearrange("(b p) m -> p b m", p=P)
        nc.sync.dma_start(amp_wide[:, 0:EARLY, 0:F], amp_blocks[:, 0:EARLY, :])
        offsets = held.tile([P, N // 16], U16, name="offsets")
        nc.sync.dma_start(offsets[:], offs)
        tables = []
        for b in range(BLOCKS):
            table = held.tile([P, S], F32, name=f"table{b}")
            nc.sync.dma_start(table[:], x[b * P : (b + 1) * P, :])
            tables.append(table)
            if b == 0:
                nc.sync.dma_start(amp_wide[:, EARLY:BLOCKS, 0:F], amp_blocks[:, EARLY:BLOCKS, :])

        identity = held.tile([P, P], F32, name="identity")
        nc.vector.memset(identity[:], 0.0)
        make_identity(nc, identity[:], nomemset=True)
        position = held.tile([P, S + QUARTER], F32, name="position")
        nc.gpsimd.iota(position[:, 0 : QUARTER + HALF], pattern=[[1, QUARTER + HALF]], base=-QUARTER, channel_multiplier=0,
                       allow_small_or_imprecise_dtypes=True)
        nc.gpsimd.iota(position[:, QUARTER + HALF :], pattern=[[1, HALF]], base=-HALF, channel_multiplier=0,
                       allow_small_or_imprecise_dtypes=True)
        sine = held.tile([P, S + QUARTER], F32, name="sine")
        nc.scalar.activation(out=sine[:], in_=position[:], func=ACT.Sin, scale=TWO_PI / S)
        minus_cos_a = sine[:, 0:S]
        sin_a = sine[:, QUARTER : QUARTER + S]
        minus_quarter_turn = held.tile([P, 1], F32, name="minus_quarter_turn")
        nc.vector.memset(minus_quarter_turn[:], -TWO_PI / 4)
        nc.vector.memset(amp_wide[:, :, F : 2 * F], 0.0)
        wave = held.tile([P, HALF], F32, name="wave")
        nc.vector.memset(wave[F:P, :], 0.0)

        freq_all = flipped.tile([P, F], F32, name="freq_all")
        nc.tensor.transpose(out=freq_all[:], in_=freq_col[:].to_broadcast([F, P]), identity=identity[0:F, 0:F])
        trig = held.tile([P, 2, F], F32, name="trig")
        nc.scalar.activation(out=trig[:, 0, :], in_=freq_all[:], func=ACT.Sin, scale=TWO_PI, bias=minus_quarter_turn[:])
        nc.scalar.activation(out=trig[:, 1, :], in_=freq_all[:], func=ACT.Sin, scale=TWO_PI)
        minus_p_q = held.tile([P, 2], F32, name="minus_p_q")
        terms = held.tile([P, 2, F], F32, name="terms")
        for k in range(2):
            nc.vector.scalar_tensor_tensor(out=terms[:, k, :], in0=amp_wide[:, 0, 0:F], scalar=1.0, in1=trig[:, k, :],
                                           op0=ALU.mult, op1=ALU.mult, accum_out=minus_p_q[:, k : k + 1])
        p_cos = held.tile([P, S], F32, name="p_cos")
        coefs = [held.tile([P, S], F32, name="coef0")]
        halves = (slice(0, HALF), slice(HALF, S))
        for half in halves:
            nc.vector.tensor_scalar(out=p_cos[:, half], in0=minus_cos_a[:, half], scalar1=minus_p_q[:, 0:1], scalar2=None, op0=ALU.mult)
        for half in halves:
            nc.vector.scalar_tensor_tensor(out=coefs[0][:, half], in0=sin_a[:, half], scalar=minus_p_q[:, 1:2], in1=p_cos[:, half],
                                           op0=ALU.mult, op1=ALU.add)

        minus_th = held.tile([F, 1], F32, name="minus_th")
        nc.gpsimd.tensor_scalar(out=minus_th[:], in0=freq_col[:], scalar1=-TWO_PI, scalar2=None, op0=ALU.mult)
        nc.scalar.activation(out=wave[0:F, :], in_=position[0:F, QUARTER : QUARTER + HALF], func=ACT.Sin, scale=TWO_PI / S, bias=minus_th[:])

        for b in range(1, BLOCKS):
            amp_t_psum = flipped.tile([P, P], F32, name="amp_t_psum")
            nc.tensor.transpose(out=amp_t_psum[:], in_=amp_wide[:, b, :], identity=identity[:])
            amp_t = held.tile([P, P], F32, name=f"amp_t{b}")
            nc.scalar.copy(out=amp_t[:], in_=amp_t_psum[:])
            coef_psum = sums.tile([P, HALF], F32, name="coef_psum")
            nc.tensor.matmul(out=coef_psum[:], lhsT=amp_t[:], rhs=wave[:], start=True, stop=True)
            coef = held.tile([P, S], F32, name=f"coef{b}")
            nc.scalar.copy(out=coef[:, 0:QUARTER], in_=coef_psum[:, QUARTER:HALF])
            nc.scalar.mul(coef[:, QUARTER : QUARTER + HALF], coef_psum[:], -1.0)
            nc.scalar.copy(out=coef[:, QUARTER + HALF : S], in_=coef_psum[:, 0:QUARTER])
            coefs.append(coef)

        def look_up(b, product, start, j, n):
            nc.vector.tensor_tensor(out=product[:, j - start : j - start + n],
                                    in0=tables[b][:].indirect(offsets[:, j // 16 : (j + n) // 16]),
                                    in1=coefs[b][:, j % S : j % S + n], op=ALU.mult)

        for b in range(BLOCKS):
            widths = [N] if b < BLOCKS - 1 else [S, S, S, HALF, HALF]
            start = 0
            for width in widths:
                product = products.tile([P, width], F32, name="product")
                pieces = [(j, min(S, width)) for j in range(start, start + width, S)]
                if b == 0:
                    pieces = [(0, HALF), (S, HALF), (HALF, HALF), (S + HALF, HALF), *pieces[2:]]
                for j, n in pieces:
                    look_up(b, product, start, j, n)
                nc.sync.dma_start(out[b * P : (b + 1) * P, start : start + width], product[:])
                start += width
